import numpy as np
import ml_dtypes


def mxq(x, axis, fmt="e4m3"):
    dtype, down = {"e4m3": (ml_dtypes.float8_e4m3fn, 7), "e5m2": (ml_dtypes.float8_e5m2, 14)}[fmt]
    v = np.moveaxis(np.asarray(x, np.float32).astype(ml_dtypes.bfloat16).astype(np.float64), axis, -1)
    blocks = v.reshape(v.shape[:-1] + (-1, 32))
    amax = np.abs(blocks).max(-1, keepdims=True)
    byte = np.maximum(np.where(amax > 0, np.frexp(amax)[1] - 1 + 127, 0) - down, 1)
    scale = np.exp2(byte - 127.0)
    codes = (blocks / scale).astype(np.float32).astype(dtype).astype(np.float64)
    return np.moveaxis((codes * scale).reshape(v.shape), -1, axis)


WIDE = False


def mx_kscale(k):
    if not WIDE:
        return np.ones(k)
    levels = np.array([10, -10, 5, -5, 0])
    if k % 512:
        return np.exp2(np.random.permutation(np.resize(levels, k // 32))).repeat(32)
    a = np.empty((k // 512, 16))
    for p in range(k // 512):
        a[p, :8] = np.random.permutation(np.resize(levels, 8))
        for g in range(8):
            far = levels[np.abs(levels - a[p, g]) >= 10]
            a[p, g + 8] = far[np.random.randint(len(far))]
    return np.exp2(a.ravel()).repeat(32)


BF16 = ml_dtypes.bfloat16


def bf(x):
    return np.asarray(x, np.float32).astype(BF16)


def f64(x):
    return np.asarray(x).astype(np.float64)


B, S, D, DV, NS, SD = 4, 1024, 1024, 512, 2, 128
R = B * S


def silu(v):
    return v / (1.0 + np.exp(-v))


def setup_inputs():
    s, r, t = mx_kscale(D), mx_kscale(D), mx_kscale(DV)
    return {"x": bf(np.random.standard_normal((B, S, D)) * r),
            "h": bf(np.random.standard_normal((B, S, D)) * s),
            "Wv": bf(np.random.standard_normal((NS, DV, D)) / np.sqrt(D) * t[:, None] / s),
            "W1": bf(np.random.standard_normal((NS, SD, D + DV)) / np.sqrt(D + DV) / np.concatenate([r, t]))}


def reference(x, h, Wv, W1):
    xf = f64(x).reshape(R, D)
    hf = f64(h).reshape(R, D)
    w1 = f64(W1)
    views = mxq(hf, 1, "e4m3") @ mxq(f64(Wv).transpose(0, 2, 1), 1, "e4m3")
    a = mxq(xf, 1, "e4m3") @ mxq(w1[:, :, :D].transpose(0, 2, 1), 1, "e4m3")
    b = mxq(views, 2, "e4m3") @ mxq(w1[:, :, D:].transpose(0, 2, 1), 1, "e4m3")
    return silu(a + b).reshape(NS, B, S, SD)

@@ -1,0 +1,201 @@
+from contextlib import ExitStack
+
+import concourse.masks as masks
+import concourse.mybir as mybir
+
+F32 = mybir.dt.float32
+BF16 = mybir.dt.bfloat16
+U32 = mybir.dt.uint32
+U8 = mybir.dt.uint8
+FP8X4 = mybir.dt.float8_e4m3fn_x4
+SILU = mybir.ActivationFunctionType.Silu
+
+P = 128
+R, D, DV, NS, SD = 4096, 1024, 512, 2, 128
+NSTEP = 16
+LAG = 2
+RAW_BUFS = 8
+FLOPS = 2 * R * NS * (D * DV + D * SD + DV * SD)
+
+START = (("h", 0), ("wv", 0), ("wv", 1), ("wv", 2), ("wv", 3), ("h", 1))
+
+
+def run_units(i):
+    units = [("h", n) for n in (i + 1, i + 2) if n < NSTEP]
+    units.append(("x", i - 1))
+    if i == 1:
+        units.append(("w1", 0))
+    units.append(("x", i))
+    return units
+
+
+def tile_distributedb_pa_t_kernel(tc, x, h, Wv, W1, out):
+    nc = tc.nc
+    rows = {
+        "x": x.rearrange("b (i p j) d -> (b i) p (j d)", p=P, j=2),
+        "h": h.rearrange("b (i p j) d -> (b i) p (j d)", p=P, j=2),
+    }
+    out_steps = out.rearrange("k b (i p j) f -> (b i) p k (j f)", p=P, j=2)
+    wv_rows = Wv.rearrange("k (m u e) d -> k u m (e d)", u=2, e=2)
+    w1_rows = W1.rearrange("k s d -> s k d")
+
+    with ExitStack() as ctx:
+        const = ctx.enter_context(tc.tile_pool(name="const", bufs=1))
+        raw_pool = ctx.enter_context(tc.tile_pool(name="raw", bufs=RAW_BUFS))
+        grp = ctx.enter_context(tc.tile_pool(name="grp", bufs=4))
+        cod = ctx.enter_context(tc.tile_pool(name="cod", bufs=5))
+        res = ctx.enter_context(tc.tile_pool(name="res", bufs=3))
+        psum = ctx.enter_context(tc.psum_pool(name="psum", bufs=8))
+        ctx.enter_context(tc.manual_schedule())
+
+        copies = (nc.vector.tensor_copy, nc.scalar.copy)
+
+        ident = const.tile([P, P], F32, name="ident")
+        masks.make_identity(nc, ident[:])
+        warm = const.tile([P, 8], F32, name="warm")
+        nc.vector.memset(warm[:], 0.0)
+        nc.scalar.activation(out=warm[:], in_=warm[:], func=SILU)
+
+        raw = {}
+        grouped = {}
+        quantised = {}
+
+        def load(unit):
+            kind, n = unit
+            if kind == "w1":
+                t = const.tile([P, 3072], BF16, name="w1_raw")
+                nc.sync.dma_start(out=t[:].rearrange("p (k d) -> p k d", k=NS), in_=w1_rows)
+            elif kind == "wv":
+                t = const.tile([P, 2048], BF16, name="wv_raw%d" % n)
+                nc.sync.dma_start(out=t[:], in_=wv_rows[n // 2, n % 2])
+            else:
+                t = raw_pool.tile([P, 2048], BF16, name=kind + "_raw", tag=kind + "_raw")
+                nc.sync.dma_start(out=t[:], in_=rows[kind][n, :, :])
+            raw[unit] = t
+
+        def flip(words, pitch, g, copy, dest):
+            bank = psum.tile([P, 2, 256], F32, name="bank", tag="bank")
+            for u in range(2):
+                for s in range(2):
+                    c0 = pitch * s + 2 * P * g
+                    nc.tensor.transpose(bank[:, u, s * P:(s + 1) * P], words[:, c0 + u:c0 + 2 * P:2], ident[:])
+            copy(out=dest, in_=bank[:].rearrange("p u r -> p r u"))
+
+        def quantise(src, codes, scales):
+            nc.vector.quantize_mx(out=codes.bitcast(FP8X4), scales=scales, in_=src)
+
+        def run(units):
+            jobs = []
+            for unit in units:
+                kind, n = unit
+                if kind == "w1":
+                    t = const.tile([P, 3072], BF16, name="w1_grp", align_bytes=64)
+                elif kind == "wv":
+                    t = const.tile([P, 2048], BF16, name="wv_grp%d" % n, align_bytes=64)
+                else:
+                    t = grp.tile([P, 2048], BF16, name=kind + "_grp", tag=kind + "_grp", align_bytes=64)
+                grouped[unit] = t
+                dest = t[:].bitcast(F32).rearrange("p (b r u) -> p b r u", r=256, u=2)
+                words = raw[unit][:].bitcast(F32)
+                for g in range(3 if kind == "w1" else 2):
+                    jobs.append((words, 768 if kind == "w1" else 512, g, dest[:, g]))
+            for n, job in enumerate(jobs):
+                flip(job[0], job[1], job[2], copies[n % 2], job[3])
+            for unit in units:
+                kind, n = unit
+                if kind in ("x", "h") and n + RAW_BUFS < NSTEP:
+                    load((kind, n + RAW_BUFS))
+            for unit in units:
+                kind, n = unit
+                if kind == "w1":
+                    codes = const.tile([P, 768], U32, name="w1_c", align_bytes=64)
+                    scales = const.tile([P, 768], U8, name="w1_s", align_bytes=64)
+                    for g in range(3):
+                        quantise(grouped[unit][:, 1024 * g:1024 * (g + 1)],
+                                 codes[:, 256 * g:256 * (g + 1)], scales[:, 256 * g:256 * (g + 1)])
+                else:
+                    if kind == "wv":
+                        codes = const.tile([P, 512], U32, name="wv_c%d" % n, align_bytes=64)
+                        scales = const.tile([P, 512], U8, name="wv_s%d" % n, align_bytes=64)
+                    else:
+                        codes = cod.tile([P, 512], U32, name=kind + "_c", tag=kind + "_c", align_bytes=64)
+                        scales = cod.tile([P, 512], U8, name=kind + "_s", tag=kind + "_s", align_bytes=64)
+                    quantise(grouped[unit][:], codes[:], scales[:])
+                quantised[unit] = (codes, scales)
+
+        def mx(acc, a, a_col, b, b_col, n, start, stop):
+            nc.tensor.matmul_mx(
+                out=acc,
+                lhsT=a[0][:, a_col:a_col + P].bitcast(FP8X4),
+                lhsT_scale=a[1][:, a_col:a_col + P],
+                rhs=b[0][:, b_col:b_col + n].bitcast(FP8X4),
+                rhs_scale=b[1][:, b_col:b_col + n],
+                start=start,
+                stop=stop,
+            )
+
+        def views(i):
+            h_q = quantised[("h", i)]
+            t = grp.tile([P, 2048], BF16, name="v_grp", tag="v_grp", align_bytes=64)
+            codes = cod.tile([P, 512], U32, name="v_c", tag="v_c", align_bytes=64)
+            scales = cod.tile([P, 512], U8, name="v_s", tag="v_s", align_bytes=64)
+            for k in range(NS):
+                flat = grp.tile([P, 4, 256], BF16, name="v_flat", tag="v_flat")
+                for th in range(2):
+                    acc = psum.tile([P, 2, 256], F32, name="v_acc", tag="bank")
+                    for t2 in range(2):
+                        for g in range(2):
+                            mx(acc[:, t2, :], quantised[("wv", 2 * k + th)], 256 * g + P * t2,
+                               h_q, 256 * g, 256, g == 0, g == 1)
+                    nc.scalar.copy(out=flat[:, 2 * th:2 * th + 2, :], in_=acc[:])
+                nc.vector.tensor_copy(
+                    out=t[:, 1024 * k:1024 * (k + 1)].rearrange("p (c i t) -> p c t i", i=4, t=4),
+                    in_=flat[:].rearrange("p t (c i) -> p c t i", i=4),
+                )
+                if i == NSTEP - 1:
+                    quantise(t[:, 1024 * k:1024 * (k + 1)], codes[:, 256 * k:256 * (k + 1)], scales[:, 256 * k:256 * (k + 1)])
+            if i < NSTEP - 1:
+                quantise(t[:], codes[:], scales[:])
+            quantised[("v", i)] = (codes, scales)
+
+        def products(acc, i, j):
+            x_q = quantised[("x", i)]
+            v_q = quantised[("v", i)]
+            w1_q = quantised[("w1", 0)]
+            for g in range(2):
+                mx(acc.rearrange("p k f -> p (k f)"), x_q, 256 * g + P * j, w1_q, 256 * g, 256, g == 0, False)
+            for k in range(NS):
+                mx(acc[:, k, :], v_q, P * (2 * k + j), w1_q, 512 + P * k, P, False, k == NS - 1)
+
+        def finish(i):
+            if i < NSTEP - 1:
+                acc = psum.tile([P, 2, NS, SD], F32, name="o_acc", tag="bank")
+                for j in range(2):
+                    products(acc[:, j, :, :], i, j)
+                o_sb = res.tile([P, NS, 2, SD], F32, name="o_sb", tag="o_sb")
+                nc.scalar.activation(out=o_sb[:], in_=acc[:].rearrange("p j k f -> p k j f"), func=SILU)
+                nc.sync.dma_start(out=out_steps[i, :, :, :], in_=o_sb[:].rearrange("p k j f -> p k (j f)"))
+            else:
+                for j in range(2):
+                    acc = psum.tile([P, NS, SD], F32, name="o_half_acc", tag="bank")
+                    products(acc[:], i, j)
+                    o_half = res.tile([P, NS, SD], F32, name="o_half", tag="o_half")
+                    nc.scalar.activation(out=o_half[:], in_=acc[:], func=SILU)
+                    nc.sync.dma_start(out=out_steps[i, :, :, SD * j:SD * (j + 1)], in_=o_half[:])
+
+        in_order_of_use = list(START)
+        for i in range(1, NSTEP, 2):
+            in_order_of_use.extend(run_units(i))
+        for unit in in_order_of_use:
+            if unit[0] in ("wv", "w1") or unit[1] < RAW_BUFS:
+                load(unit)
+
+        for unit in START:
+            run([unit])
+        for i in range(NSTEP + LAG):
+            if i % 2 == 1 and i < NSTEP:
+                run(run_units(i))
+            if i < NSTEP:
+                views(i)
+            if i >= LAG:
+                finish(i - LAG)

@@ -13,42 +13,31 @@ SILU = mybir.ActivationFunctionType.Silu
 P = 128
 R, D, DV, NS, SD = 4096, 1024, 512, 2, 128
 NSTEP = 16
-LAG = 2
 RAW_BUFS = 8
 FLOPS = 2 * R * NS * (D * DV + D * SD + DV * SD)
-
-START = (("h", 0), ("wv", 0), ("wv", 1), ("wv", 2), ("wv", 3), ("h", 1))
-
-
-def run_units(i):
-    units = [("h", n) for n in (i + 1, i + 2) if n < NSTEP]
-    units.append(("x", i - 1))
-    if i == 1:
-        units.append(("w1", 0))
-    units.append(("x", i))
-    return units
 
 
 def tile_distributedb_pa_t_kernel(tc, x, h, Wv, W1, out):
     nc = tc.nc
     rows = {
-        "x": x.rearrange("b (i p j) d -> (b i) p (j d)", p=P, j=2),
-        "h": h.rearrange("b (i p j) d -> (b i) p (j d)", p=P, j=2),
+        "x": x.rearrange("b (i p s) d -> (b i) p (s d)", p=P, s=2),
+        "h": h.rearrange("b (i p s) d -> (b i) p (s d)", p=P, s=2),
     }
-    out_steps = out.rearrange("k b (i p j) f -> (b i) p k (j f)", p=P, j=2)
-    wv_rows = Wv.rearrange("k (m u e) d -> k u m (e d)", u=2, e=2)
-    w1_rows = W1.rearrange("k s d -> s k d")
+    wv_rows = Wv.rearrange("k (m n e) d -> k n m (e d)", n=2, e=2)
+    w1_rows = W1.rearrange("k f d -> f k d")
+    out_steps = out.rearrange("k b (i p s) f -> (b i) p k (s f)", p=P, s=2)
 
     with ExitStack() as ctx:
         const = ctx.enter_context(tc.tile_pool(name="const", bufs=1))
         raw_pool = ctx.enter_context(tc.tile_pool(name="raw", bufs=RAW_BUFS))
-        grp = ctx.enter_context(tc.tile_pool(name="grp", bufs=4))
-        cod = ctx.enter_context(tc.tile_pool(name="cod", bufs=5))
+        srt = ctx.enter_context(tc.tile_pool(name="srt", bufs=3))
+        grp = ctx.enter_context(tc.tile_pool(name="grp", bufs=3))
+        cod = ctx.enter_context(tc.tile_pool(name="cod", bufs=4))
         res = ctx.enter_context(tc.tile_pool(name="res", bufs=3))
         psum = ctx.enter_context(tc.psum_pool(name="psum", bufs=8))
         ctx.enter_context(tc.manual_schedule())
 
-        copies = (nc.vector.tensor_copy, nc.scalar.copy)
+        copies = (nc.scalar.copy, nc.vector.tensor_copy)
 
         ident = const.tile([P, P], F32, name="ident")
         masks.make_identity(nc, ident[:])
@@ -57,6 +46,7 @@ def tile_distributedb_pa_t_kernel(tc, x, h, Wv, W1, out):
         nc.scalar.activation(out=warm[:], in_=warm[:], func=SILU)
 
         raw = {}
+        columns = {}
         grouped = {}
         quantised = {}
 
@@ -65,27 +55,34 @@ def tile_distributedb_pa_t_kernel(tc, x, h, Wv, W1, out):
             if kind == "w1":
                 t = const.tile([P, 3072], BF16, name="w1_raw")
                 nc.sync.dma_start(out=t[:].rearrange("p (k d) -> p k d", k=NS), in_=w1_rows)
+                pitch = 768
             elif kind == "wv":
                 t = const.tile([P, 2048], BF16, name="wv_raw%d" % n)
                 nc.sync.dma_start(out=t[:], in_=wv_rows[n // 2, n % 2])
+                pitch = 512
             else:
                 t = raw_pool.tile([P, 2048], BF16, name=kind + "_raw", tag=kind + "_raw")
                 nc.sync.dma_start(out=t[:], in_=rows[kind][n, :, :])
-            raw[unit] = t
+                pitch = 512
+            words = t[:].bitcast(F32)
+            raw[unit] = words
+            columns[unit] = lambda s, g, u: words[:, pitch * s + 256 * g + u:pitch * s + 256 * (g + 1):2]
 
-        def flip(words, pitch, g, copy, dest):
-            bank = psum.tile([P, 2, 256], F32, name="bank", tag="bank")
-            for u in range(2):
-                for s in range(2):
-                    c0 = pitch * s + 2 * P * g
-                    nc.tensor.transpose(bank[:, u, s * P:(s + 1) * P], words[:, c0 + u:c0 + 2 * P:2], ident[:])
-            copy(out=dest, in_=bank[:].rearrange("p u r -> p r u"))
+        def sort(unit):
+            kind, n = unit
+            if unit not in raw:
+                return
+            t = srt.tile([P, 1024], F32, name=kind + "_srt", tag=kind + "_srt")
+            nc.vector.tensor_copy(
+                out=t[:].rearrange("p (c u q) -> p c u q", u=2, q=P),
+                in_=raw[unit].rearrange("p (c q u) -> p c u q", u=2, q=P),
+            )
+            columns[unit] = lambda s, g, u: t[:, 512 * s + 256 * g + P * u:512 * s + 256 * g + P * (u + 1)]
+            if n + RAW_BUFS < NSTEP:
+                load((kind, n + RAW_BUFS))
 
-        def quantise(src, codes, scales):
-            nc.vector.quantize_mx(out=codes.bitcast(FP8X4), scales=scales, in_=src)
-
-        def run(units):
-            jobs = []
+        def flip(units, pattern="SV"):
+            n_bank = 0
             for unit in units:
                 kind, n = unit
                 if kind == "w1":
@@ -95,33 +92,37 @@ def tile_distributedb_pa_t_kernel(tc, x, h, Wv, W1, out):
                 else:
                     t = grp.tile([P, 2048], BF16, name=kind + "_grp", tag=kind + "_grp", align_bytes=64)
                 grouped[unit] = t
-                dest = t[:].bitcast(F32).rearrange("p (b r u) -> p b r u", r=256, u=2)
-                words = raw[unit][:].bitcast(F32)
+                dest = t[:].bitcast(F32).rearrange("p (g r u) -> p g r u", r=256, u=2)
                 for g in range(3 if kind == "w1" else 2):
-                    jobs.append((words, 768 if kind == "w1" else 512, g, dest[:, g]))
-            for n, job in enumerate(jobs):
-                flip(job[0], job[1], job[2], copies[n % 2], job[3])
-            for unit in units:
-                kind, n = unit
-                if kind in ("x", "h") and n + RAW_BUFS < NSTEP:
-                    load((kind, n + RAW_BUFS))
-            for unit in units:
-                kind, n = unit
-                if kind == "w1":
-                    codes = const.tile([P, 768], U32, name="w1_c", align_bytes=64)
-                    scales = const.tile([P, 768], U8, name="w1_s", align_bytes=64)
-                    for g in range(3):
-                        quantise(grouped[unit][:, 1024 * g:1024 * (g + 1)],
-                                 codes[:, 256 * g:256 * (g + 1)], scales[:, 256 * g:256 * (g + 1)])
+                    bank = psum.tile([P, 2, 256], F32, name="bank", tag="bank")
+                    for u in range(2):
+                        for s in range(2):
+                            nc.tensor.transpose(bank[:, u, s * P:(s + 1) * P], columns[unit](s, g, u), ident[:])
+                    copies["SV".index(pattern[n_bank % len(pattern)])](out=dest[:, g], in_=bank[:].rearrange("p u r -> p r u"))
+                    n_bank += 1
+
+        def quantise_columns(src, codes, scales):
+            nc.vector.quantize_mx(out=codes.bitcast(FP8X4), scales=scales, in_=src)
+
+        def quantise(unit):
+            kind, n = unit
+            if unit not in grouped:
+                return
+            if kind == "w1":
+                codes = const.tile([P, 768], U32, name="w1_c", align_bytes=64)
+                scales = const.tile([P, 768], U8, name="w1_s", align_bytes=64)
+                for g in range(3):
+                    quantise_columns(grouped[unit][:, 1024 * g:1024 * (g + 1)],
+                                     codes[:, 256 * g:256 * (g + 1)], scales[:, 256 * g:256 * (g + 1)])
+            else:
+                if kind == "wv":
+                    codes = const.tile([P, 512], U32, name="wv_c%d" % n, align_bytes=64)
+                    scales = const.tile([P, 512], U8, name="wv_s%d" % n, align_bytes=64)
                 else:
-                    if kind == "wv":
-                        codes = const.tile([P, 512], U32, name="wv_c%d" % n, align_bytes=64)
-                        scales = const.tile([P, 512], U8, name="wv_s%d" % n, align_bytes=64)
-                    else:
-                        codes = cod.tile([P, 512], U32, name=kind + "_c", tag=kind + "_c", align_bytes=64)
-                        scales = cod.tile([P, 512], U8, name=kind + "_s", tag=kind + "_s", align_bytes=64)
-                    quantise(grouped[unit][:], codes[:], scales[:])
-                quantised[unit] = (codes, scales)
+                    codes = cod.tile([P, 512], U32, name=kind + "_c", tag=kind + "_c", align_bytes=64)
+                    scales = cod.tile([P, 512], U8, name=kind + "_s", tag=kind + "_s", align_bytes=64)
+                quantise_columns(grouped[unit][:], codes[:], scales[:])
+            quantised[unit] = (codes, scales)
 
         def mx(acc, a, a_col, b, b_col, n, start, stop):
             nc.tensor.matmul_mx(
@@ -134,68 +135,97 @@ def tile_distributedb_pa_t_kernel(tc, x, h, Wv, W1, out):
                 stop=stop,
             )
 
-        def views(i):
-            h_q = quantised[("h", i)]
-            t = grp.tile([P, 2048], BF16, name="v_grp", tag="v_grp", align_bytes=64)
-            codes = cod.tile([P, 512], U32, name="v_c", tag="v_c", align_bytes=64)
-            scales = cod.tile([P, 512], U8, name="v_s", tag="v_s", align_bytes=64)
-            for k in range(NS):
-                flat = grp.tile([P, 4, 256], BF16, name="v_flat", tag="v_flat")
-                for th in range(2):
-                    acc = psum.tile([P, 2, 256], F32, name="v_acc", tag="bank")
-                    for t2 in range(2):
-                        for g in range(2):
-                            mx(acc[:, t2, :], quantised[("wv", 2 * k + th)], 256 * g + P * t2,
-                               h_q, 256 * g, 256, g == 0, g == 1)
-                    nc.scalar.copy(out=flat[:, 2 * th:2 * th + 2, :], in_=acc[:])
-                nc.vector.tensor_copy(
-                    out=t[:, 1024 * k:1024 * (k + 1)].rearrange("p (c i t) -> p c t i", i=4, t=4),
-                    in_=flat[:].rearrange("p t (c i) -> p c t i", i=4),
-                )
-                if i == NSTEP - 1:
-                    quantise(t[:, 1024 * k:1024 * (k + 1)], codes[:, 256 * k:256 * (k + 1)], scales[:, 256 * k:256 * (k + 1)])
-            if i < NSTEP - 1:
-                quantise(t[:], codes[:], scales[:])
-            quantised[("v", i)] = (codes, scales)
+        def views(i, k):
+            unit = ("v", i)
+            if k == 0:
+                t_grp = grp.tile([P, 2048], BF16, name="v_grp", tag="v_grp", align_bytes=64)
+                grouped[unit] = t_grp
+            dest = grouped[unit][:].rearrange("p (k s r t) -> p k s r t", k=NS, s=2, t=4)
+            for s in range(2):
+                acc = psum.tile([P, 4, P], F32, name="v_acc", tag="bank")
+                for t in range(4):
+                    for g in range(2):
+                        mx(acc[:, t, :], quantised[("wv", 2 * k + t // 2)], 256 * g + P * (t % 2),
+                           quantised[("h", i)], 256 * g + P * s, P, g == 0, g == 1)
+                nc.scalar.copy(out=dest[:, k, s], in_=acc[:].rearrange("p t r -> p r t"))
 
-        def products(acc, i, j):
+        def finish(i):
             x_q = quantised[("x", i)]
             v_q = quantised[("v", i)]
             w1_q = quantised[("w1", 0)]
-            for g in range(2):
-                mx(acc.rearrange("p k f -> p (k f)"), x_q, 256 * g + P * j, w1_q, 256 * g, 256, g == 0, False)
-            for k in range(NS):
-                mx(acc[:, k, :], v_q, P * (2 * k + j), w1_q, 512 + P * k, P, False, k == NS - 1)
+            acc = psum.tile([P, 2, NS, SD], F32, name="o_acc", tag="bank")
+            for s in range(2):
+                for g in range(2):
+                    mx(acc[:, s].rearrange("p k f -> p (k f)"), x_q, 256 * g + P * s, w1_q, 256 * g, 256, g == 0, False)
+                for k in range(NS):
+                    mx(acc[:, s, k, :], v_q, P * (2 * k + s), w1_q, 512 + P * k, P, False, k == NS - 1)
+            o_sb = res.tile([P, NS, 2, SD], F32, name="o_sb", tag="o_sb")
+            nc.scalar.activation(out=o_sb[:], in_=acc[:].rearrange("p s k f -> p k s f"), func=SILU)
+            nc.sync.dma_start(out=out_steps[i, :, :, :], in_=o_sb[:].rearrange("p k s f -> p k (s f)"))
 
-        def finish(i):
-            if i < NSTEP - 1:
-                acc = psum.tile([P, 2, NS, SD], F32, name="o_acc", tag="bank")
-                for j in range(2):
-                    products(acc[:, j, :, :], i, j)
-                o_sb = res.tile([P, NS, 2, SD], F32, name="o_sb", tag="o_sb")
-                nc.scalar.activation(out=o_sb[:], in_=acc[:].rearrange("p j k f -> p k j f"), func=SILU)
-                nc.sync.dma_start(out=out_steps[i, :, :, :], in_=o_sb[:].rearrange("p k j f -> p k (j f)"))
-            else:
-                for j in range(2):
-                    acc = psum.tile([P, NS, SD], F32, name="o_half_acc", tag="bank")
-                    products(acc[:], i, j)
-                    o_half = res.tile([P, NS, SD], F32, name="o_half", tag="o_half")
-                    nc.scalar.activation(out=o_half[:], in_=acc[:], func=SILU)
-                    nc.sync.dma_start(out=out_steps[i, :, :, SD * j:SD * (j + 1)], in_=o_half[:])
+        for unit in (("wv", 0), ("wv", 1), ("h", 0), ("h", 1), ("wv", 2), ("wv", 3), ("x", 0), ("h", 2), ("w1", 0)):
+            load(unit)
+        for n in range(1, RAW_BUFS):
+            if n + 2 < RAW_BUFS:
+                load(("h", n + 2))
+            load(("x", n))
 
-        in_order_of_use = list(START)
-        for i in range(1, NSTEP, 2):
-            in_order_of_use.extend(run_units(i))
-        for unit in in_order_of_use:
-            if unit[0] in ("wv", "w1") or unit[1] < RAW_BUFS:
-                load(unit)
-
-        for unit in START:
-            run([unit])
-        for i in range(NSTEP + LAG):
-            if i % 2 == 1 and i < NSTEP:
-                run(run_units(i))
-            if i < NSTEP:
-                views(i)
-            if i >= LAG:
-                finish(i - LAG)
+        flip([("wv", 0)])
+        quantise(("wv", 0))
+        flip([("wv", 1)])
+        quantise(("wv", 1))
+        flip([("h", 0)])
+        quantise(("h", 0))
+        flip([("h", 1)])
+        load(("h", RAW_BUFS))
+        load(("h", RAW_BUFS + 1))
+        flip([("wv", 2)])
+        views(0, 0)
+        quantise(("h", 1))
+        quantise(("wv", 2))
+        sort(("x", 0))
+        views(1, 0)
+        flip([("wv", 3)])
+        quantise(("wv", 3))
+        sort(("h", 2))
+        flip([("x", 0), ("h", 2)])
+        quantise(("x", 0))
+        views(0, 1)
+        quantise(("h", 2))
+        sort(("h", 3))
+        sort(("x", 1))
+        flip([("w1", 0)])
+        quantise(("w1", 0))
+        quantise(("v", 0))
+        views(1, 1)
+        finish(0)
+        quantise(("v", 1))
+        flip([("h", 3), ("x", 1)])
+        quantise(("x", 1))
+        quantise(("h", 3))
+        for i in range(4, 6):
+            sort(("h", i))
+        for i in range(2, 4):
+            sort(("x", i))
+        views(2, 0)
+        views(2, 1)
+        finish(1)
+        for i in range(3, NSTEP, 2):
+            quantise(("v", i - 1))
+            flip([u for u in (("h", i + 1), ("h", i + 2), ("x", i - 1), ("x", i)) if u[1] < NSTEP])
+            quantise(("h", i + 1))
+            quantise(("x", i - 1))
+            sort(("h", i + 3))
+            views(i, 0)
+            views(i, 1)
+            finish(i - 1)
+            quantise(("h", i + 2))
+            quantise(("x", i))
+            quantise(("v", i))
+            sort(("h", i + 4))
+            sort(("x", i + 1))
+            sort(("x", i + 2))
+            if i + 1 < NSTEP:
+                views(i + 1, 0)
+                views(i + 1, 1)
+            finish(i)

@@ -68,17 +68,18 @@ def tile_distributedb_pa_t_kernel(tc, x, h, Wv, W1, out):
             raw[unit] = words
             columns[unit] = lambda s, g, u: words[:, pitch * s + 256 * g + u:pitch * s + 256 * (g + 1):2]
 
-        def sort(unit):
+        def sort(unit, eng=None):
             kind, n = unit
             if unit not in raw:
                 return
-            t = srt.tile([P, 1024], F32, name=kind + "_srt", tag=kind + "_srt")
-            nc.vector.tensor_copy(
+            pitch = 768 if kind == "w1" else 512
+            t = srt.tile([P, 2 * pitch], F32, name=kind + "_srt", tag=kind + "_srt")
+            (eng or nc.vector.tensor_copy)(
                 out=t[:].rearrange("p (c u q) -> p c u q", u=2, q=P),
                 in_=raw[unit].rearrange("p (c q u) -> p c u q", u=2, q=P),
             )
-            columns[unit] = lambda s, g, u: t[:, 512 * s + 256 * g + P * u:512 * s + 256 * g + P * (u + 1)]
-            if n + RAW_BUFS < NSTEP:
+            columns[unit] = lambda s, g, u: t[:, pitch * s + 256 * g + P * u:pitch * s + 256 * g + P * (u + 1)]
+            if kind in ("x", "h") and n + RAW_BUFS < NSTEP:
                 load((kind, n + RAW_BUFS))
 
         def flip(units, pattern="SV"):
@@ -124,6 +125,16 @@ def tile_distributedb_pa_t_kernel(tc, x, h, Wv, W1, out):
                 quantise_columns(grouped[unit][:], codes[:], scales[:])
             quantised[unit] = (codes, scales)
 
+        def quantise_views(i, k, s):
+            unit = ("v", i)
+            if unit not in quantised:
+                codes = cod.tile([P, 512], U32, name="v_c", tag="v_c", align_bytes=64)
+                scales = cod.tile([P, 512], U8, name="v_s", tag="v_s", align_bytes=64)
+                quantised[unit] = (codes, scales)
+            codes, scales = quantised[unit]
+            c0 = P * (2 * k + s)
+            quantise_columns(grouped[unit][:, 4 * c0:4 * (c0 + P)], codes[:, c0:c0 + P], scales[:, c0:c0 + P])
+
         def mx(acc, a, a_col, b, b_col, n, start, stop):
             nc.tensor.matmul_mx(
                 out=acc,
@@ -135,13 +146,13 @@ def tile_distributedb_pa_t_kernel(tc, x, h, Wv, W1, out):
                 stop=stop,
             )
 
-        def views(i, k):
+        def views(i, k, tiles=(0, 1)):
             unit = ("v", i)
-            if k == 0:
+            if unit not in grouped:
                 t_grp = grp.tile([P, 2048], BF16, name="v_grp", tag="v_grp", align_bytes=64)
                 grouped[unit] = t_grp
             dest = grouped[unit][:].rearrange("p (k s r t) -> p k s r t", k=NS, s=2, t=4)
-            for s in range(2):
+            for s in tiles:
                 acc = psum.tile([P, 4, P], F32, name="v_acc", tag="bank")
                 for t in range(4):
                     for g in range(2):
@@ -149,16 +160,26 @@ def tile_distributedb_pa_t_kernel(tc, x, h, Wv, W1, out):
                            quantised[("h", i)], 256 * g + P * s, P, g == 0, g == 1)
                 nc.scalar.copy(out=dest[:, k, s], in_=acc[:].rearrange("p t r -> p r t"))
 
-        def finish(i):
+        def products(acc, i, s):
             x_q = quantised[("x", i)]
             v_q = quantised[("v", i)]
             w1_q = quantised[("w1", 0)]
+            for g in range(2):
+                mx(acc.rearrange("p k f -> p (k f)"), x_q, 256 * g + P * s, w1_q, 256 * g, 256, g == 0, False)
+            for k in range(NS):
+                mx(acc[:, k, :], v_q, P * (2 * k + s), w1_q, 512 + P * k, P, False, k == NS - 1)
+
+        def finish_half(i, s):
+            acc = psum.tile([P, NS, SD], F32, name="o_half_acc", tag="bank")
+            products(acc[:], i, s)
+            o_half = res.tile([P, NS, SD], F32, name="o_half", tag="o_half")
+            nc.scalar.activation(out=o_half[:], in_=acc[:], func=SILU)
+            nc.sync.dma_start(out=out_steps[i, :, :, SD * s:SD * (s + 1)], in_=o_half[:])
+
+        def finish(i):
             acc = psum.tile([P, 2, NS, SD], F32, name="o_acc", tag="bank")
             for s in range(2):
-                for g in range(2):
-                    mx(acc[:, s].rearrange("p k f -> p (k f)"), x_q, 256 * g + P * s, w1_q, 256 * g, 256, g == 0, False)
-                for k in range(NS):
-                    mx(acc[:, s, k, :], v_q, P * (2 * k + s), w1_q, 512 + P * k, P, False, k == NS - 1)
+                products(acc[:, s], i, s)
             o_sb = res.tile([P, NS, 2, SD], F32, name="o_sb", tag="o_sb")
             nc.scalar.activation(out=o_sb[:], in_=acc[:].rearrange("p s k f -> p k s f"), func=SILU)
             nc.sync.dma_start(out=out_steps[i, :, :, :], in_=o_sb[:].rearrange("p k s f -> p k (s f)"))
@@ -183,11 +204,11 @@ def tile_distributedb_pa_t_kernel(tc, x, h, Wv, W1, out):
         views(0, 0)
         quantise(("h", 1))
         quantise(("wv", 2))
-        sort(("x", 0))
-        views(1, 0)
         flip([("wv", 3)])
-        quantise(("wv", 3))
+        sort(("x", 0))
         sort(("h", 2))
+        quantise(("wv", 3))
+        views(1, 0)
         flip([("x", 0), ("h", 2)])
         quantise(("x", 0))
         views(0, 1)
@@ -199,33 +220,45 @@ def tile_distributedb_pa_t_kernel(tc, x, h, Wv, W1, out):
         quantise(("v", 0))
         views(1, 1)
         finish(0)
-        quantise(("v", 1))
-        flip([("h", 3), ("x", 1)])
-        quantise(("x", 1))
-        quantise(("h", 3))
-        for i in range(4, 6):
-            sort(("h", i))
-        for i in range(2, 4):
-            sort(("x", i))
-        views(2, 0)
-        views(2, 1)
-        finish(1)
-        for i in range(3, NSTEP, 2):
-            quantise(("v", i - 1))
-            flip([u for u in (("h", i + 1), ("h", i + 2), ("x", i - 1), ("x", i)) if u[1] < NSTEP])
-            quantise(("h", i + 1))
-            quantise(("x", i - 1))
-            sort(("h", i + 3))
-            views(i, 0)
-            views(i, 1)
-            finish(i - 1)
-            quantise(("h", i + 2))
-            quantise(("x", i))
-            quantise(("v", i))
-            sort(("h", i + 4))
-            sort(("x", i + 1))
-            sort(("x", i + 2))
-            if i + 1 < NSTEP:
-                views(i + 1, 0)
-                views(i + 1, 1)
-            finish(i)
+        groups = ((2, 2), (4, 2), (6, 2), (8, 2), (10, 2), (12, 2), (14, 2))
+        sort(("h", 4))
+        sort(("x", 2))
+        for a, size in groups:
+            last = a + size == NSTEP
+            quantise(("v", a - 1))
+            units = []
+            for i in range(a, a + size):
+                if i + 1 < NSTEP:
+                    units.append(("h", i + 1))
+                units.append(("x", i - 1))
+            if last:
+                units.append(("x", NSTEP - 1))
+            flip(units, "SV")
+            quantise(("h", a + 1))
+            quantise(("x", a - 1))
+            for i in range(a, a + size):
+                if i < NSTEP - 1:
+                    views(i, 0)
+                    views(i, 1)
+                    finish(i - 1)
+                    if i + 1 < a + size:
+                        quantise(("h", i + 2))
+                        quantise(("x", i))
+                        quantise(("v", i))
+                    nxt = dict(groups).get(a + size, 0)
+                    for n in range(nxt * (i - a) // size, nxt * (i - a + 1) // size):
+                        if a + size + n + 1 < NSTEP:
+                            sort(("h", a + size + n + 1))
+                        sort(("x", a + size + n - 1))
+                        if a + size + n == NSTEP - 1:
+                            sort(("x", NSTEP - 1))
+        quantise(("x", NSTEP - 1))
+        for s in range(2):
+            for k in range(NS):
+                views(NSTEP - 1, k, (s,))
+        finish(NSTEP - 2)
+        for s in range(2):
+            for k in range(NS):
+                quantise_views(NSTEP - 1, k, s)
+        for s in range(2):
+            finish_half(NSTEP - 1, s)

@@ -13,7 +13,7 @@ SILU = mybir.ActivationFunctionType.Silu
 P = 128
 R, D, DV, NS, SD = 4096, 1024, 512, 2, 128
 NSTEP = 16
-RAW_BUFS = 8
+RAW_BUFS = 12
 FLOPS = 2 * R * NS * (D * DV + D * SD + DV * SD)
 
 
@@ -30,9 +30,9 @@ def tile_distributedb_pa_t_kernel(tc, x, h, Wv, W1, out):
     with ExitStack() as ctx:
         const = ctx.enter_context(tc.tile_pool(name="const", bufs=1))
         raw_pool = ctx.enter_context(tc.tile_pool(name="raw", bufs=RAW_BUFS))
-        srt = ctx.enter_context(tc.tile_pool(name="srt", bufs=3))
-        grp = ctx.enter_context(tc.tile_pool(name="grp", bufs=3))
-        cod = ctx.enter_context(tc.tile_pool(name="cod", bufs=4))
+        srt = ctx.enter_context(tc.tile_pool(name="srt", bufs=4))
+        grp = ctx.enter_context(tc.tile_pool(name="grp", bufs=4))
+        cod = ctx.enter_context(tc.tile_pool(name="cod", bufs=6))
         res = ctx.enter_context(tc.tile_pool(name="res", bufs=3))
         psum = ctx.enter_context(tc.psum_pool(name="psum", bufs=8))
         ctx.enter_context(tc.manual_schedule())
@@ -56,22 +56,28 @@ def tile_distributedb_pa_t_kernel(tc, x, h, Wv, W1, out):
                 t = const.tile([P, 3072], BF16, name="w1_raw")
                 nc.sync.dma_start(out=t[:].rearrange("p (k d) -> p k d", k=NS), in_=w1_rows)
                 pitch = 768
-            elif kind == "wv":
-                t = const.tile([P, 2048], BF16, name="wv_raw%d" % n)
-                nc.sync.dma_start(out=t[:], in_=wv_rows[n // 2, n % 2])
-                pitch = 512
             else:
-                t = raw_pool.tile([P, 2048], BF16, name=kind + "_raw", tag=kind + "_raw")
-                nc.sync.dma_start(out=t[:], in_=rows[kind][n, :, :])
+                t = raw_pool.tile([P, 2048], BF16, name="raw", tag="raw")
+                nc.sync.dma_start(out=t[:], in_=wv_rows[n // 2, n % 2] if kind == "wv" else rows[kind][n, :, :])
                 pitch = 512
             words = t[:].bitcast(F32)
             raw[unit] = words
             columns[unit] = lambda s, g, u: words[:, pitch * s + 256 * g + u:pitch * s + 256 * (g + 1):2]
 
+        stream = [("wv", 0), ("wv", 1), ("h", 0), ("h", 1), ("wv", 2), ("wv", 3), ("h", 2), ("h", 3)]
+        for n in range(NSTEP):
+            if n + 4 < NSTEP:
+                stream.append(("h", n + 4))
+            stream.append(("x", n))
+        ahead = []
+
+        def load_next():
+            if stream:
+                ahead.append(stream[0])
+                load(stream.pop(0))
+
         def sort(unit, eng=None):
             kind, n = unit
-            if unit not in raw:
-                return
             pitch = 768 if kind == "w1" else 512
             t = srt.tile([P, 2 * pitch], F32, name=kind + "_srt", tag=kind + "_srt")
             (eng or nc.vector.tensor_copy)(
@@ -79,13 +85,15 @@ def tile_distributedb_pa_t_kernel(tc, x, h, Wv, W1, out):
                 in_=raw[unit].rearrange("p (c q u) -> p c u q", u=2, q=P),
             )
             columns[unit] = lambda s, g, u: t[:, pitch * s + 256 * g + P * u:pitch * s + 256 * g + P * (u + 1)]
-            if kind in ("x", "h") and n + RAW_BUFS < NSTEP:
-                load((kind, n + RAW_BUFS))
+            load_next()
 
         def flip(units, pattern="SV"):
             n_bank = 0
+            direct = []
             for unit in units:
                 kind, n = unit
+                if kind == "wv" or unit in (("h", 0), ("h", 1)):
+                    direct.append(unit)
                 if kind == "w1":
                     t = const.tile([P, 3072], BF16, name="w1_grp", align_bytes=64)
                 elif kind == "wv":
@@ -101,6 +109,8 @@ def tile_distributedb_pa_t_kernel(tc, x, h, Wv, W1, out):
                             nc.tensor.transpose(bank[:, u, s * P:(s + 1) * P], columns[unit](s, g, u), ident[:])
                     copies["SV".index(pattern[n_bank % len(pattern)])](out=dest[:, g], in_=bank[:].rearrange("p u r -> p r u"))
                     n_bank += 1
+            for unit in direct:
+                load_next()
 
         def quantise_columns(src, codes, scales):
             nc.vector.quantize_mx(out=codes.bitcast(FP8X4), scales=scales, in_=src)
@@ -146,12 +156,35 @@ def tile_distributedb_pa_t_kernel(tc, x, h, Wv, W1, out):
                 stop=stop,
             )
 
+        def wide(i, k):
+            return i > 1
+
+        flats = {}
+
+        def regroup(i, k):
+            if (i, k) in flats:
+                nc.vector.tensor_copy(
+                    out=grouped[("v", i)][:, 1024 * k:1024 * (k + 1)].rearrange("p (c i t) -> p c t i", i=4, t=4),
+                    in_=flats[(i, k)][:].rearrange("p t (c i) -> p c t i", i=4),
+                )
+
         def views(i, k, tiles=(0, 1)):
             unit = ("v", i)
             if unit not in grouped:
                 t_grp = grp.tile([P, 2048], BF16, name="v_grp", tag="v_grp", align_bytes=64)
                 grouped[unit] = t_grp
             dest = grouped[unit][:].rearrange("p (k s r t) -> p k s r t", k=NS, s=2, t=4)
+            if len(tiles) == 2 and wide(i, k):
+                flat = grp.tile([P, 4, 256], BF16, name="v_flat", tag="v_flat")
+                flats[(i, k)] = flat
+                for n in range(2):
+                    acc = psum.tile([P, 2, 256], F32, name="v_acc", tag="bank")
+                    for e in range(2):
+                        for g in range(2):
+                            mx(acc[:, e, :], quantised[("wv", 2 * k + n)], 256 * g + P * e,
+                               quantised[("h", i)], 256 * g, 256, g == 0, g == 1)
+                    nc.scalar.copy(out=flat[:, 2 * n:2 * n + 2, :], in_=acc[:])
+                return
             for s in tiles:
                 acc = psum.tile([P, 4, P], F32, name="v_acc", tag="bank")
                 for t in range(4):
@@ -184,12 +217,11 @@ def tile_distributedb_pa_t_kernel(tc, x, h, Wv, W1, out):
             nc.scalar.activation(out=o_sb[:], in_=acc[:].rearrange("p s k f -> p k s f"), func=SILU)
             nc.sync.dma_start(out=out_steps[i, :, :, :], in_=o_sb[:].rearrange("p k s f -> p k (s f)"))
 
-        for unit in (("wv", 0), ("wv", 1), ("h", 0), ("h", 1), ("wv", 2), ("wv", 3), ("x", 0), ("h", 2), ("w1", 0)):
-            load(unit)
-        for n in range(1, RAW_BUFS):
-            if n + 2 < RAW_BUFS:
-                load(("h", n + 2))
-            load(("x", n))
+        for n in range(10):
+            load_next()
+        load(("w1", 0))
+        for n in range(2):
+            load_next()
 
         flip([("wv", 0)])
         quantise(("wv", 0))
@@ -198,64 +230,64 @@ def tile_distributedb_pa_t_kernel(tc, x, h, Wv, W1, out):
         flip([("h", 0)])
         quantise(("h", 0))
         flip([("h", 1)])
-        load(("h", RAW_BUFS))
-        load(("h", RAW_BUFS + 1))
         flip([("wv", 2)])
         views(0, 0)
         quantise(("h", 1))
         quantise(("wv", 2))
         flip([("wv", 3)])
-        sort(("x", 0))
         sort(("h", 2))
         quantise(("wv", 3))
-        views(1, 0)
-        flip([("x", 0), ("h", 2)])
-        quantise(("x", 0))
-        views(0, 1)
-        quantise(("h", 2))
         sort(("h", 3))
-        sort(("x", 1))
-        flip([("w1", 0)])
-        quantise(("w1", 0))
-        quantise(("v", 0))
-        views(1, 1)
-        finish(0)
-        groups = ((2, 2), (4, 2), (6, 2), (8, 2), (10, 2), (12, 2), (14, 2))
+        views(1, 0)
+        flip([("h", 2), ("h", 3)])
+        quantise(("h", 2))
+        views(0, 1)
         sort(("h", 4))
-        sort(("x", 2))
+        sort(("x", 0))
+        quantise(("v", 0))
+        quantise(("h", 3))
+        sort(("h", 5))
+        sort(("x", 1))
+        views(1, 1)
+        groups = ((2, 2), (4, 2), (6, 2), (8, 2), (10, 2), (12, 2), (14, 2))
         for a, size in groups:
-            last = a + size == NSTEP
-            quantise(("v", a - 1))
             units = []
             for i in range(a, a + size):
-                if i + 1 < NSTEP:
-                    units.append(("h", i + 1))
-                units.append(("x", i - 1))
-            if last:
+                if i + 2 < NSTEP:
+                    units.append(("h", i + 2))
+                units.append(("x", i - 2))
+                if i == 2:
+                    units.append(("w1", 0))
+            if a + size == NSTEP:
+                units.append(("x", NSTEP - 2))
                 units.append(("x", NSTEP - 1))
-            flip(units, "SV")
-            quantise(("h", a + 1))
-            quantise(("x", a - 1))
+            flip(units, "SSV")
             for i in range(a, a + size):
+                quantise(("x", i - 2))
+                if i == 2:
+                    quantise(("w1", 0))
+                regroup(i - 1, 0)
+                quantise(("h", i + 2))
+                regroup(i - 1, 1)
+                nxt = dict(groups).get(a + size, 0)
+                for n in range(nxt * (i - a) // size, nxt * (i - a + 1) // size):
+                    if a + size + n + 2 < NSTEP:
+                        sort(("h", a + size + n + 2))
+                    sort(("x", a + size + n - 2))
+                    if a + size + n == NSTEP - 1:
+                        sort(("x", NSTEP - 2))
+                        sort(("x", NSTEP - 1))
+                quantise(("v", i - 1))
                 if i < NSTEP - 1:
                     views(i, 0)
                     views(i, 1)
-                    finish(i - 1)
-                    if i + 1 < a + size:
-                        quantise(("h", i + 2))
-                        quantise(("x", i))
-                        quantise(("v", i))
-                    nxt = dict(groups).get(a + size, 0)
-                    for n in range(nxt * (i - a) // size, nxt * (i - a + 1) // size):
-                        if a + size + n + 1 < NSTEP:
-                            sort(("h", a + size + n + 1))
-                        sort(("x", a + size + n - 1))
-                        if a + size + n == NSTEP - 1:
-                            sort(("x", NSTEP - 1))
+                    finish(i - 2)
+        quantise(("x", NSTEP - 2))
         quantise(("x", NSTEP - 1))
         for s in range(2):
             for k in range(NS):
                 views(NSTEP - 1, k, (s,))
+        finish(NSTEP - 3)
         finish(NSTEP - 2)
         for s in range(2):
             for k in range(NS):

@@ -30,7 +30,7 @@ def tile_distributedb_pa_t_kernel(tc, x, h, Wv, W1, out):
     with ExitStack() as ctx:
         const = ctx.enter_context(tc.tile_pool(name="const", bufs=1))
         raw_pool = ctx.enter_context(tc.tile_pool(name="raw", bufs=RAW_BUFS))
-        srt = ctx.enter_context(tc.tile_pool(name="srt", bufs=4))
+        srt = ctx.enter_context(tc.tile_pool(name="srt", bufs=8))
         grp = ctx.enter_context(tc.tile_pool(name="grp", bufs=4))
         cod = ctx.enter_context(tc.tile_pool(name="cod", bufs=6))
         res = ctx.enter_context(tc.tile_pool(name="res", bufs=3))
@@ -50,6 +50,8 @@ def tile_distributedb_pa_t_kernel(tc, x, h, Wv, W1, out):
         grouped = {}
         quantised = {}
 
+        halved = (("wv", 0),)
+
         def load(unit):
             kind, n = unit
             if kind == "w1":
@@ -58,7 +60,12 @@ def tile_distributedb_pa_t_kernel(tc, x, h, Wv, W1, out):
                 pitch = 768
             else:
                 t = raw_pool.tile([P, 2048], BF16, name="raw", tag="raw")
-                nc.sync.dma_start(out=t[:], in_=wv_rows[n // 2, n % 2] if kind == "wv" else rows[kind][n, :, :])
+                source = wv_rows[n // 2, n % 2] if kind == "wv" else rows[kind][n, :, :]
+                if unit in halved:
+                    for s in range(2):
+                        nc.sync.dma_start(out=t[:, D * s:D * (s + 1)], in_=source[:, D * s:D * (s + 1)])
+                else:
+                    nc.sync.dma_start(out=t[:], in_=source)
                 pitch = 512
             words = t[:].bitcast(F32)
             raw[unit] = words
@@ -70,6 +77,7 @@ def tile_distributedb_pa_t_kernel(tc, x, h, Wv, W1, out):
                 stream.append(("h", n + 4))
             stream.append(("x", n))
         ahead = []
+        in_order = []
 
         def load_next():
             if stream:
@@ -79,20 +87,22 @@ def tile_distributedb_pa_t_kernel(tc, x, h, Wv, W1, out):
         def sort(unit, eng=None):
             kind, n = unit
             pitch = 768 if kind == "w1" else 512
-            t = srt.tile([P, 2 * pitch], F32, name=kind + "_srt", tag=kind + "_srt")
+            t = srt.tile([P, 2 * pitch], F32, name="srt", tag="srt")
             (eng or nc.vector.tensor_copy)(
                 out=t[:].rearrange("p (c u q) -> p c u q", u=2, q=P),
                 in_=raw[unit].rearrange("p (c q u) -> p c u q", u=2, q=P),
             )
             columns[unit] = lambda s, g, u: t[:, pitch * s + 256 * g + P * u:pitch * s + 256 * g + P * (u + 1)]
-            load_next()
+            in_order.append(unit)
+            if kind != "w1":
+                load_next()
 
         def flip(units, pattern="SV"):
             n_bank = 0
             direct = []
             for unit in units:
                 kind, n = unit
-                if kind == "wv" or unit in (("h", 0), ("h", 1)):
+                if kind != "w1" and unit not in in_order:
                     direct.append(unit)
                 if kind == "w1":
                     t = const.tile([P, 3072], BF16, name="w1_grp", align_bytes=64)
@@ -102,11 +112,23 @@ def tile_distributedb_pa_t_kernel(tc, x, h, Wv, W1, out):
                     t = grp.tile([P, 2048], BF16, name=kind + "_grp", tag=kind + "_grp", align_bytes=64)
                 grouped[unit] = t
                 dest = t[:].bitcast(F32).rearrange("p (g r u) -> p g r u", r=256, u=2)
+                banks = []
+                if unit in halved:
+                    for g in range(2):
+                        bank = psum.tile([P, 2, 256], F32, name="bank", tag="bank")
+                        banks.append(bank)
+                    for s in range(2):
+                        for g in range(2):
+                            for u in range(2):
+                                nc.tensor.transpose(banks[g][:, u, s * P:(s + 1) * P], columns[unit](s, g, u), ident[:])
                 for g in range(3 if kind == "w1" else 2):
-                    bank = psum.tile([P, 2, 256], F32, name="bank", tag="bank")
-                    for u in range(2):
-                        for s in range(2):
-                            nc.tensor.transpose(bank[:, u, s * P:(s + 1) * P], columns[unit](s, g, u), ident[:])
+                    if unit in halved:
+                        bank = banks[g]
+                    else:
+                        bank = psum.tile([P, 2, 256], F32, name="bank", tag="bank")
+                        for u in range(2):
+                            for s in range(2):
+                                nc.tensor.transpose(bank[:, u, s * P:(s + 1) * P], columns[unit](s, g, u), ident[:])
                     copies["SV".index(pattern[n_bank % len(pattern)])](out=dest[:, g], in_=bank[:].rearrange("p u r -> p r u"))
                     n_bank += 1
             for unit in direct:
@@ -164,8 +186,8 @@ def tile_distributedb_pa_t_kernel(tc, x, h, Wv, W1, out):
         def regroup(i, k):
             if (i, k) in flats:
                 nc.vector.tensor_copy(
-                    out=grouped[("v", i)][:, 1024 * k:1024 * (k + 1)].rearrange("p (c i t) -> p c t i", i=4, t=4),
-                    in_=flats[(i, k)][:].rearrange("p t (c i) -> p c t i", i=4),
+                    out=grouped[("v", i)][:, 1024 * k:1024 * (k + 1)].bitcast(F32).rearrange("p (r n) -> p r n", n=2),
+                    in_=flats[(i, k)][:].rearrange("p n r e -> p (n r e)").bitcast(F32).rearrange("p (n r) -> p r n", n=2),
                 )
 
         def views(i, k, tiles=(0, 1)):
@@ -175,7 +197,7 @@ def tile_distributedb_pa_t_kernel(tc, x, h, Wv, W1, out):
                 grouped[unit] = t_grp
             dest = grouped[unit][:].rearrange("p (k s r t) -> p k s r t", k=NS, s=2, t=4)
             if len(tiles) == 2 and wide(i, k):
-                flat = grp.tile([P, 4, 256], BF16, name="v_flat", tag="v_flat")
+                flat = grp.tile([P, 2, 256, 2], BF16, name="v_flat", tag="v_flat")
                 flats[(i, k)] = flat
                 for n in range(2):
                     acc = psum.tile([P, 2, 256], F32, name="v_acc", tag="bank")
@@ -183,7 +205,7 @@ def tile_distributedb_pa_t_kernel(tc, x, h, Wv, W1, out):
                         for g in range(2):
                             mx(acc[:, e, :], quantised[("wv", 2 * k + n)], 256 * g + P * e,
                                quantised[("h", i)], 256 * g, 256, g == 0, g == 1)
-                    nc.scalar.copy(out=flat[:, 2 * n:2 * n + 2, :], in_=acc[:])
+                    nc.scalar.copy(out=flat[:, n], in_=acc[:].rearrange("p e r -> p r e"))
                 return
             for s in tiles:
                 acc = psum.tile([P, 4, P], F32, name="v_acc", tag="bank")
@@ -261,7 +283,7 @@ def tile_distributedb_pa_t_kernel(tc, x, h, Wv, W1, out):
             if a + size == NSTEP:
                 units.append(("x", NSTEP - 2))
                 units.append(("x", NSTEP - 1))
-            flip(units, "SSV")
+            flip(units, "SVSSVSSV")
             for i in range(a, a + size):
                 quantise(("x", i - 2))
                 if i == 2:

@@ -32,7 +32,7 @@ def tile_distributedb_pa_t_kernel(tc, x, h, Wv, W1, out):
         raw_pool = ctx.enter_context(tc.tile_pool(name="raw", bufs=RAW_BUFS))
         srt = ctx.enter_context(tc.tile_pool(name="srt", bufs=8))
         grp = ctx.enter_context(tc.tile_pool(name="grp", bufs=4))
-        cod = ctx.enter_context(tc.tile_pool(name="cod", bufs=6))
+        cod = ctx.enter_context(tc.tile_pool(name="cod", bufs=4))
         res = ctx.enter_context(tc.tile_pool(name="res", bufs=3))
         psum = ctx.enter_context(tc.psum_pool(name="psum", bufs=8))
         ctx.enter_context(tc.manual_schedule())
@@ -87,7 +87,10 @@ def tile_distributedb_pa_t_kernel(tc, x, h, Wv, W1, out):
         def sort(unit, eng=None):
             kind, n = unit
             pitch = 768 if kind == "w1" else 512
-            t = srt.tile([P, 2 * pitch], F32, name="srt", tag="srt")
+            if kind == "w1":
+                t = const.tile([P, 2 * pitch], F32, name="w1_srt")
+            else:
+                t = srt.tile([P, 2 * pitch], F32, name="srt", tag="srt")
             (eng or nc.vector.tensor_copy)(
                 out=t[:].rearrange("p (c u q) -> p c u q", u=2, q=P),
                 in_=raw[unit].rearrange("p (c q u) -> p c u q", u=2, q=P),
@@ -152,8 +155,8 @@ def tile_distributedb_pa_t_kernel(tc, x, h, Wv, W1, out):
                     codes = const.tile([P, 512], U32, name="wv_c%d" % n, align_bytes=64)
                     scales = const.tile([P, 512], U8, name="wv_s%d" % n, align_bytes=64)
                 else:
-                    codes = cod.tile([P, 512], U32, name=kind + "_c", tag=kind + "_c", align_bytes=64)
-                    scales = cod.tile([P, 512], U8, name=kind + "_s", tag=kind + "_s", align_bytes=64)
+                    codes = cod.tile([P, 512], U32, name=kind + "_c", tag=kind + "_c", align_bytes=64, bufs=6 if kind == "h" else 4)
+                    scales = cod.tile([P, 512], U8, name=kind + "_s", tag=kind + "_s", align_bytes=64, bufs=6 if kind == "h" else 4)
                 quantise_columns(grouped[unit][:], codes[:], scales[:])
             quantised[unit] = (codes, scales)
 
@@ -253,17 +256,19 @@ def tile_distributedb_pa_t_kernel(tc, x, h, Wv, W1, out):
         quantise(("h", 0))
         flip([("h", 1)])
         flip([("wv", 2)])
+        sort(("wv", 3), nc.scalar.copy)
         views(0, 0)
         quantise(("h", 1))
         quantise(("wv", 2))
         flip([("wv", 3)])
         sort(("h", 2))
         quantise(("wv", 3))
-        sort(("h", 3))
+        sort(("h", 3), nc.scalar.copy)
         views(1, 0)
         flip([("h", 2), ("h", 3)])
         quantise(("h", 2))
         views(0, 1)
+        sort(("w1", 0), nc.scalar.copy)
         sort(("h", 4))
         sort(("x", 0))
         quantise(("v", 0))

@@ -13,6 +13,7 @@ SILU = mybir.ActivationFunctionType.Silu
 P = 128
 R, D, DV, NS, SD = 4096, 1024, 512, 2, 128
 NSTEP = 16
+LAST = NSTEP - 1
 RAW_BUFS = 12
 FLOPS = 2 * R * NS * (D * DV + D * SD + DV * SD)
 
@@ -31,13 +32,14 @@ def tile_distributedb_pa_t_kernel(tc, x, h, Wv, W1, out):
         const = ctx.enter_context(tc.tile_pool(name="const", bufs=1))
         raw_pool = ctx.enter_context(tc.tile_pool(name="raw", bufs=RAW_BUFS))
         srt = ctx.enter_context(tc.tile_pool(name="srt", bufs=8))
-        grp = ctx.enter_context(tc.tile_pool(name="grp", bufs=4))
-        cod = ctx.enter_context(tc.tile_pool(name="cod", bufs=4))
+        grp = ctx.enter_context(tc.tile_pool(name="grp", bufs=2))
+        vgrp = ctx.enter_context(tc.tile_pool(name="vgrp", bufs=3))
+        cod = ctx.enter_context(tc.tile_pool(name="cod", bufs=3))
         res = ctx.enter_context(tc.tile_pool(name="res", bufs=3))
         psum = ctx.enter_context(tc.psum_pool(name="psum", bufs=8))
         ctx.enter_context(tc.manual_schedule())
 
-        copies = (nc.scalar.copy, nc.vector.tensor_copy)
+        copies = {"S": nc.scalar.copy, "V": nc.vector.tensor_copy}
 
         ident = const.tile([P, P], F32, name="ident")
         masks.make_identity(nc, ident[:])
@@ -48,9 +50,8 @@ def tile_distributedb_pa_t_kernel(tc, x, h, Wv, W1, out):
         raw = {}
         columns = {}
         grouped = {}
-        quantised = {}
-
-        halved = (("wv", 0),)
+        codes_of = {}
+        flats = {}
 
         def load(unit):
             kind, n = unit
@@ -61,178 +62,176 @@ def tile_distributedb_pa_t_kernel(tc, x, h, Wv, W1, out):
             else:
                 t = raw_pool.tile([P, 2048], BF16, name="raw", tag="raw")
                 source = wv_rows[n // 2, n % 2] if kind == "wv" else rows[kind][n, :, :]
-                if unit in halved:
-                    for s in range(2):
-                        nc.sync.dma_start(out=t[:, D * s:D * (s + 1)], in_=source[:, D * s:D * (s + 1)])
-                else:
-                    nc.sync.dma_start(out=t[:], in_=source)
+                pieces = 4 if unit == ("wv", 0) else 1
+                width = 2048 // pieces
+                for j in range(pieces):
+                    nc.sync.dma_start(out=t[:, width * j:width * (j + 1)], in_=source[:, width * j:width * (j + 1)])
                 pitch = 512
             words = t[:].bitcast(F32)
             raw[unit] = words
             columns[unit] = lambda s, g, u: words[:, pitch * s + 256 * g + u:pitch * s + 256 * (g + 1):2]
 
         stream = [("wv", 0), ("wv", 1), ("h", 0), ("h", 1), ("wv", 2), ("wv", 3), ("h", 2), ("h", 3)]
-        for n in range(NSTEP):
+        for n in range(0, NSTEP, 2):
+            stream.extend([("x", n), ("x", n + 1)])
             if n + 4 < NSTEP:
-                stream.append(("h", n + 4))
-            stream.append(("x", n))
-        ahead = []
-        in_order = []
+                stream.extend([("h", n + 4), ("h", n + 5)])
 
-        def load_next():
-            if stream:
-                ahead.append(stream[0])
-                load(stream.pop(0))
+        def load_next(count):
+            for unit in stream[:count]:
+                load(unit)
+            stream[:count] = []
 
-        def sort(unit, eng=None):
-            kind, n = unit
-            pitch = 768 if kind == "w1" else 512
-            if kind == "w1":
+        def sort(unit, copy=nc.vector.tensor_copy):
+            if unit[0] == "w1":
+                pitch = 768
                 t = const.tile([P, 2 * pitch], F32, name="w1_srt")
             else:
+                pitch = 512
                 t = srt.tile([P, 2 * pitch], F32, name="srt", tag="srt")
-            (eng or nc.vector.tensor_copy)(
+            copy(
                 out=t[:].rearrange("p (c u q) -> p c u q", u=2, q=P),
                 in_=raw[unit].rearrange("p (c q u) -> p c u q", u=2, q=P),
             )
             columns[unit] = lambda s, g, u: t[:, pitch * s + 256 * g + P * u:pitch * s + 256 * g + P * (u + 1)]
-            in_order.append(unit)
-            if kind != "w1":
-                load_next()
+            if unit[0] != "w1":
+                load_next(1)
 
         def flip(units, pattern="SV"):
             n_bank = 0
-            direct = []
             for unit in units:
                 kind, n = unit
-                if kind != "w1" and unit not in in_order:
-                    direct.append(unit)
-                if kind == "w1":
-                    t = const.tile([P, 3072], BF16, name="w1_grp", align_bytes=64)
-                elif kind == "wv":
-                    t = const.tile([P, 2048], BF16, name="wv_grp%d" % n, align_bytes=64)
+                groups = 3 if kind == "w1" else 2
+                if kind in ("x", "h"):
+                    pair = (kind, n // 2)
+                    if pair not in grouped:
+                        t = grp.tile([P, 4096], BF16, name=kind + "_grp", tag=kind + "_grp", align_bytes=64)
+                        grouped[pair] = t
+                    dest = grouped[pair][:, 2048 * (n % 2):2048 * (n % 2 + 1)]
                 else:
-                    t = grp.tile([P, 2048], BF16, name=kind + "_grp", tag=kind + "_grp", align_bytes=64)
-                grouped[unit] = t
-                dest = t[:].bitcast(F32).rearrange("p (g r u) -> p g r u", r=256, u=2)
+                    t = const.tile([P, 1024 * groups], BF16, name="%s_grp%d" % unit, align_bytes=64)
+                    grouped[unit] = t
+                    dest = t[:]
+                dest = dest.bitcast(F32).rearrange("p (g r u) -> p g r u", r=256, u=2)
                 banks = []
-                if unit in halved:
-                    for g in range(2):
-                        bank = psum.tile([P, 2, 256], F32, name="bank", tag="bank")
-                        banks.append(bank)
-                    for s in range(2):
-                        for g in range(2):
-                            for u in range(2):
-                                nc.tensor.transpose(banks[g][:, u, s * P:(s + 1) * P], columns[unit](s, g, u), ident[:])
-                for g in range(3 if kind == "w1" else 2):
-                    if unit in halved:
-                        bank = banks[g]
-                    else:
-                        bank = psum.tile([P, 2, 256], F32, name="bank", tag="bank")
+                for g in range(groups):
+                    bank = psum.tile([P, 2, 256], F32, name="bank", tag="bank")
+                    banks.append(bank)
+                if unit == ("wv", 0):
+                    order = [(s, g, u) for s in range(2) for g in range(groups) for u in range(2)]
+                    for s, g, u in order:
+                        nc.tensor.transpose(banks[g][:, u, s * P:(s + 1) * P], columns[unit](s, g, u), ident[:])
+                for g in range(groups):
+                    if unit != ("wv", 0):
                         for u in range(2):
                             for s in range(2):
-                                nc.tensor.transpose(bank[:, u, s * P:(s + 1) * P], columns[unit](s, g, u), ident[:])
-                    copies["SV".index(pattern[n_bank % len(pattern)])](out=dest[:, g], in_=bank[:].rearrange("p u r -> p r u"))
+                                nc.tensor.transpose(banks[g][:, u, s * P:(s + 1) * P], columns[unit](s, g, u), ident[:])
+                    copies[pattern[n_bank % len(pattern)]](out=dest[:, g], in_=banks[g][:].rearrange("p u r -> p r u"))
                     n_bank += 1
-            for unit in direct:
-                load_next()
 
         def quantise_columns(src, codes, scales):
             nc.vector.quantize_mx(out=codes.bitcast(FP8X4), scales=scales, in_=src)
 
+        def code_tiles(kind, unit):
+            if kind in ("x", "h"):
+                codes = cod.tile([P, 1024], U32, name=kind + "_c", tag=kind + "_c", align_bytes=64)
+                scales = cod.tile([P, 1024], U8, name=kind + "_s", tag=kind + "_s", align_bytes=64)
+            elif kind == "v":
+                codes = cod.tile([P, 512], U32, name="v_c", tag="v_c", align_bytes=64)
+                scales = cod.tile([P, 512], U8, name="v_s", tag="v_s", align_bytes=64)
+            else:
+                width = 768 if kind == "w1" else 512
+                codes = const.tile([P, width], U32, name="%s_c%d" % unit, align_bytes=64)
+                scales = const.tile([P, width], U8, name="%s_s%d" % unit, align_bytes=64)
+            codes_of[unit] = (codes, scales)
+            return codes, scales
+
         def quantise(unit):
             kind, n = unit
-            if unit not in grouped:
-                return
+            codes, scales = code_tiles(kind, unit)
             if kind == "w1":
-                codes = const.tile([P, 768], U32, name="w1_c", align_bytes=64)
-                scales = const.tile([P, 768], U8, name="w1_s", align_bytes=64)
-                for g in range(3):
-                    quantise_columns(grouped[unit][:, 1024 * g:1024 * (g + 1)],
-                                     codes[:, 256 * g:256 * (g + 1)], scales[:, 256 * g:256 * (g + 1)])
+                for c in range(0, 768, 256):
+                    quantise_columns(grouped[unit][:, 4 * c:4 * c + 1024], codes[:, c:c + 256], scales[:, c:c + 256])
             else:
-                if kind == "wv":
-                    codes = const.tile([P, 512], U32, name="wv_c%d" % n, align_bytes=64)
-                    scales = const.tile([P, 512], U8, name="wv_s%d" % n, align_bytes=64)
-                else:
-                    codes = cod.tile([P, 512], U32, name=kind + "_c", tag=kind + "_c", align_bytes=64, bufs=6 if kind == "h" else 4)
-                    scales = cod.tile([P, 512], U8, name=kind + "_s", tag=kind + "_s", align_bytes=64, bufs=6 if kind == "h" else 4)
                 quantise_columns(grouped[unit][:], codes[:], scales[:])
-            quantised[unit] = (codes, scales)
+
+        def quantise_half(pair, j):
+            if pair not in codes_of:
+                code_tiles(pair[0], pair)
+            codes, scales = codes_of[pair]
+            quantise_columns(grouped[pair][:, 2048 * j:2048 * (j + 1)], codes[:, 512 * j:512 * (j + 1)], scales[:, 512 * j:512 * (j + 1)])
 
         def quantise_views(i, k, s):
             unit = ("v", i)
-            if unit not in quantised:
-                codes = cod.tile([P, 512], U32, name="v_c", tag="v_c", align_bytes=64)
-                scales = cod.tile([P, 512], U8, name="v_s", tag="v_s", align_bytes=64)
-                quantised[unit] = (codes, scales)
-            codes, scales = quantised[unit]
+            if unit not in codes_of:
+                code_tiles("v", unit)
+            codes, scales = codes_of[unit]
             c0 = P * (2 * k + s)
             quantise_columns(grouped[unit][:, 4 * c0:4 * (c0 + P)], codes[:, c0:c0 + P], scales[:, c0:c0 + P])
 
-        def mx(acc, a, a_col, b, b_col, n, start, stop):
-            nc.tensor.matmul_mx(
-                out=acc,
-                lhsT=a[0][:, a_col:a_col + P].bitcast(FP8X4),
-                lhsT_scale=a[1][:, a_col:a_col + P],
-                rhs=b[0][:, b_col:b_col + n].bitcast(FP8X4),
-                rhs_scale=b[1][:, b_col:b_col + n],
-                start=start,
-                stop=stop,
-            )
+        def codes_at(kind, i, col, width):
+            if kind in ("x", "h"):
+                codes, scales = codes_of[(kind, i // 2)]
+                col += 512 * (i % 2)
+            else:
+                codes, scales = codes_of[(kind, i)]
+            return codes[:, col:col + width].bitcast(FP8X4), scales[:, col:col + width]
 
-        def wide(i, k):
-            return i > 1
+        def mx(acc, a, b, start, stop):
+            nc.tensor.matmul_mx(out=acc, lhsT=a[0], lhsT_scale=a[1], rhs=b[0], rhs_scale=b[1], start=start, stop=stop)
 
-        flats = {}
-
-        def regroup(i, k):
-            if (i, k) in flats:
-                nc.vector.tensor_copy(
-                    out=grouped[("v", i)][:, 1024 * k:1024 * (k + 1)].bitcast(F32).rearrange("p (r n) -> p r n", n=2),
-                    in_=flats[(i, k)][:].rearrange("p n r e -> p (n r e)").bitcast(F32).rearrange("p (n r) -> p r n", n=2),
-                )
+        def views_tile(i):
+            t = vgrp.tile([P, 2048], BF16, name="v_grp", tag="v_grp", align_bytes=64)
+            grouped[("v", i)] = t
 
         def views(i, k, tiles=(0, 1)):
-            unit = ("v", i)
-            if unit not in grouped:
-                t_grp = grp.tile([P, 2048], BF16, name="v_grp", tag="v_grp", align_bytes=64)
-                grouped[unit] = t_grp
-            dest = grouped[unit][:].rearrange("p (k s r t) -> p k s r t", k=NS, s=2, t=4)
-            if len(tiles) == 2 and wide(i, k):
-                flat = grp.tile([P, 2, 256, 2], BF16, name="v_flat", tag="v_flat")
-                flats[(i, k)] = flat
-                for n in range(2):
-                    acc = psum.tile([P, 2, 256], F32, name="v_acc", tag="bank")
-                    for e in range(2):
-                        for g in range(2):
-                            mx(acc[:, e, :], quantised[("wv", 2 * k + n)], 256 * g + P * e,
-                               quantised[("h", i)], 256 * g, 256, g == 0, g == 1)
-                    nc.scalar.copy(out=flat[:, n], in_=acc[:].rearrange("p e r -> p r e"))
-                return
+            if ("v", i) not in grouped:
+                views_tile(i)
+            dest = grouped[("v", i)][:].rearrange("p (k s r t) -> p k s r t", k=NS, s=2, t=4)
             for s in tiles:
                 acc = psum.tile([P, 4, P], F32, name="v_acc", tag="bank")
                 for t in range(4):
                     for g in range(2):
-                        mx(acc[:, t, :], quantised[("wv", 2 * k + t // 2)], 256 * g + P * (t % 2),
-                           quantised[("h", i)], 256 * g + P * s, P, g == 0, g == 1)
+                        mx(acc[:, t, :], codes_at("wv", 2 * k + t // 2, 256 * g + P * (t % 2), P),
+                           codes_at("h", i, 256 * g + P * s, P), g == 0, g == 1)
                 nc.scalar.copy(out=dest[:, k, s], in_=acc[:].rearrange("p t r -> p r t"))
 
-        def products(acc, i, s):
-            x_q = quantised[("x", i)]
-            v_q = quantised[("v", i)]
-            w1_q = quantised[("w1", 0)]
-            for g in range(2):
-                mx(acc.rearrange("p k f -> p (k f)"), x_q, 256 * g + P * s, w1_q, 256 * g, 256, g == 0, False)
+        def wide_views(i):
+            flat = vgrp.tile([P, NS, 2, 256, 2], BF16, name="v_flat", tag="v_flat", bufs=2)
+            flats[i] = flat
             for k in range(NS):
-                mx(acc[:, k, :], v_q, P * (2 * k + s), w1_q, 512 + P * k, P, False, k == NS - 1)
+                for n in range(2):
+                    acc = psum.tile([P, 2, 256], F32, name="v_acc", tag="bank")
+                    for e in range(2):
+                        for g in range(2):
+                            mx(acc[:, e, :], codes_at("wv", 2 * k + n, 256 * g + P * e, P),
+                               codes_at("h", i, 256 * g, 256), g == 0, g == 1)
+                    nc.scalar.copy(out=flat[:, k, n], in_=acc[:].rearrange("p e r -> p r e"))
 
-        def finish_half(i, s):
-            acc = psum.tile([P, NS, SD], F32, name="o_half_acc", tag="bank")
-            products(acc[:], i, s)
-            o_half = res.tile([P, NS, SD], F32, name="o_half", tag="o_half")
-            nc.scalar.activation(out=o_half[:], in_=acc[:], func=SILU)
-            nc.sync.dma_start(out=out_steps[i, :, :, SD * s:SD * (s + 1)], in_=o_half[:])
+        def regroup(i):
+            if i in flats:
+                views_tile(i)
+                nc.vector.tensor_copy(
+                    out=grouped[("v", i)][:].bitcast(F32).rearrange("p (k r n) -> p k r n", k=NS, n=2),
+                    in_=flats[i][:].rearrange("p k n r e -> p (k n r e)").bitcast(F32).rearrange("p (k n r) -> p k r n", k=NS, n=2),
+                )
+
+        def products(acc, i, s, subnets=(0, 1)):
+            k0 = subnets[0]
+            for g in range(2):
+                mx(acc.rearrange("p k f -> p (k f)"), codes_at("x", i, 256 * g + P * s, P),
+                   codes_at("w1", 0, 256 * g + P * k0, P * len(subnets)), g == 0, False)
+            for k in subnets:
+                mx(acc[:, k - k0, :], codes_at("v", i, P * (2 * k + s), P), codes_at("w1", 0, 512 + P * k, P),
+                   False, k == subnets[-1])
+
+        def finish_part(i, s, subnets=(0, 1)):
+            k0, n = subnets[0], len(subnets)
+            acc = psum.tile([P, n, SD], F32, name="o_part_acc", tag="bank")
+            products(acc[:], i, s, subnets)
+            o_part = res.tile([P, n, SD], F32, name="o_part", tag="o_part", bufs=6)
+            nc.scalar.activation(out=o_part[:], in_=acc[:], func=SILU)
+            nc.sync.dma_start(out=out_steps[i, :, k0:k0 + n, SD * s:SD * (s + 1)], in_=o_part[:])
 
         def finish(i):
             acc = psum.tile([P, 2, NS, SD], F32, name="o_acc", tag="bank")
@@ -242,82 +241,84 @@ def tile_distributedb_pa_t_kernel(tc, x, h, Wv, W1, out):
             nc.scalar.activation(out=o_sb[:], in_=acc[:].rearrange("p s k f -> p k s f"), func=SILU)
             nc.sync.dma_start(out=out_steps[i, :, :, :], in_=o_sb[:].rearrange("p k s f -> p k (s f)"))
 
-        for n in range(10):
-            load_next()
+        load_next(10)
         load(("w1", 0))
-        for n in range(2):
-            load_next()
+        load_next(2)
 
         flip([("wv", 0)])
         quantise(("wv", 0))
         flip([("wv", 1)])
         quantise(("wv", 1))
         flip([("h", 0)])
-        quantise(("h", 0))
+        quantise_half(("h", 0), 0)
         flip([("h", 1)])
+        load_next(4)
         flip([("wv", 2)])
+        load_next(1)
         sort(("wv", 3), nc.scalar.copy)
         views(0, 0)
-        quantise(("h", 1))
+        quantise_half(("h", 0), 1)
         quantise(("wv", 2))
         flip([("wv", 3)])
+
         sort(("h", 2))
         quantise(("wv", 3))
         sort(("h", 3), nc.scalar.copy)
         views(1, 0)
         flip([("h", 2), ("h", 3)])
-        quantise(("h", 2))
+        quantise_half(("h", 1), 0)
         views(0, 1)
         sort(("w1", 0), nc.scalar.copy)
-        sort(("h", 4))
         sort(("x", 0))
-        quantise(("v", 0))
-        quantise(("h", 3))
-        sort(("h", 5))
         sort(("x", 1))
+        quantise(("v", 0))
+        quantise_half(("h", 1), 1)
+        sort(("h", 4))
+        sort(("h", 5))
         views(1, 1)
-        groups = ((2, 2), (4, 2), (6, 2), (8, 2), (10, 2), (12, 2), (14, 2))
-        for a, size in groups:
-            units = []
-            for i in range(a, a + size):
-                if i + 2 < NSTEP:
-                    units.append(("h", i + 2))
-                units.append(("x", i - 2))
-                if i == 2:
-                    units.append(("w1", 0))
-            if a + size == NSTEP:
-                units.append(("x", NSTEP - 2))
-                units.append(("x", NSTEP - 1))
+        for a in range(2, NSTEP, 2):
+            regroup(a - 1)
+            units = [("x", a - 2), ("x", a - 1)]
+            if a == 2:
+                units.append(("w1", 0))
+            if a + 2 < NSTEP:
+                units.extend([("h", a + 2), ("h", a + 3)])
+            else:
+                units.extend([("x", a), ("x", a + 1)])
             flip(units, "SVSSVSSV")
-            for i in range(a, a + size):
-                quantise(("x", i - 2))
-                if i == 2:
-                    quantise(("w1", 0))
-                regroup(i - 1, 0)
-                quantise(("h", i + 2))
-                regroup(i - 1, 1)
-                nxt = dict(groups).get(a + size, 0)
-                for n in range(nxt * (i - a) // size, nxt * (i - a + 1) // size):
-                    if a + size + n + 2 < NSTEP:
-                        sort(("h", a + size + n + 2))
-                    sort(("x", a + size + n - 2))
-                    if a + size + n == NSTEP - 1:
-                        sort(("x", NSTEP - 2))
-                        sort(("x", NSTEP - 1))
-                quantise(("v", i - 1))
-                if i < NSTEP - 1:
-                    views(i, 0)
-                    views(i, 1)
-                    finish(i - 2)
-        quantise(("x", NSTEP - 2))
-        quantise(("x", NSTEP - 1))
-        for s in range(2):
-            for k in range(NS):
-                views(NSTEP - 1, k, (s,))
-        finish(NSTEP - 3)
-        finish(NSTEP - 2)
-        for s in range(2):
-            for k in range(NS):
-                quantise_views(NSTEP - 1, k, s)
-        for s in range(2):
-            finish_half(NSTEP - 1, s)
+            quantise(("x", a // 2 - 1))
+            if a == 2:
+                quantise(("w1", 0))
+            quantise(("v", a - 1))
+            later = []
+            if a + 2 < NSTEP:
+                later.extend([("x", a), ("x", a + 1)])
+                later.extend([("h", a + 4), ("h", a + 5)] if a + 4 < NSTEP else [("x", a + 2), ("x", a + 3)])
+            wide_views(a)
+            for unit in later[:2]:
+                sort(unit)
+            regroup(a)
+            finish(a - 2)
+            for unit in later[2:]:
+                sort(unit)
+            if a + 2 < NSTEP:
+                quantise(("h", a // 2 + 1))
+                quantise(("v", a))
+                wide_views(a + 1)
+                finish(a - 1)
+        quantise(("v", LAST - 1))
+        quantise(("x", LAST // 2))
+        for k in range(NS):
+            views(LAST, k, (0,))
+        finish(LAST - 2)
+        for k in range(NS):
+            quantise_views(LAST, k, 0)
+        for k in range(NS):
+            views(LAST, k, (1,))
+        finish_part(LAST, 0)
+        for k in range(NS):
+            quantise_views(LAST, k, 1)
+        finish_part(LAST - 1, 0)
+        finish_part(LAST - 1, 1)
+        finish_part(LAST, 1, (0,))
+        finish_part(LAST, 1, (1,))

from contextlib import ExitStack

import concourse.masks as masks
import concourse.mybir as mybir

F32 = mybir.dt.float32
BF16 = mybir.dt.bfloat16
U32 = mybir.dt.uint32
U8 = mybir.dt.uint8
FP8X4 = mybir.dt.float8_e4m3fn_x4
SILU = mybir.ActivationFunctionType.Silu

P = 128
R, D, DV, NS, SD = 4096, 1024, 512, 2, 128
NSTEP = 16
LAST = NSTEP - 1
RAW_BUFS = 12
FLOPS = 2 * R * NS * (D * DV + D * SD + DV * SD)


def tile_distributedb_pa_t_kernel(tc, x, h, Wv, W1, out):
    nc = tc.nc
    rows = {
        "x": x.rearrange("b (i p s) d -> (b i) p (s d)", p=P, s=2),
        "h": h.rearrange("b (i p s) d -> (b i) p (s d)", p=P, s=2),
    }
    wv_rows = Wv.rearrange("k (m n e) d -> k n m (e d)", n=2, e=2)
    w1_rows = W1.rearrange("k f d -> f k d")
    out_steps = out.rearrange("k b (i p s) f -> (b i) p k (s f)", p=P, s=2)

    with ExitStack() as ctx:
        const = ctx.enter_context(tc.tile_pool(name="const", bufs=1))
        raw_pool = ctx.enter_context(tc.tile_pool(name="raw", bufs=RAW_BUFS))
        srt = ctx.enter_context(tc.tile_pool(name="srt", bufs=8))
        grp = ctx.enter_context(tc.tile_pool(name="grp", bufs=2))
        vgrp = ctx.enter_context(tc.tile_pool(name="vgrp", bufs=3))
        cod = ctx.enter_context(tc.tile_pool(name="cod", bufs=3))
        res = ctx.enter_context(tc.tile_pool(name="res", bufs=3))
        psum = ctx.enter_context(tc.psum_pool(name="psum", bufs=8))
        ctx.enter_context(tc.manual_schedule())

        copies = {"S": nc.scalar.copy, "V": nc.vector.tensor_copy}

        ident = const.tile([P, P], F32, name="ident")
        masks.make_identity(nc, ident[:])
        warm = const.tile([P, 8], F32, name="warm")
        nc.vector.memset(warm[:], 0.0)
        nc.scalar.activation(out=warm[:], in_=warm[:], func=SILU)

        raw = {}
        columns = {}
        grouped = {}
        codes_of = {}
        flats = {}

        def load(unit):
            kind, n = unit
            if kind == "w1":
                t = const.tile([P, 3072], BF16, name="w1_raw")
                nc.sync.dma_start(out=t[:].rearrange("p (k d) -> p k d", k=NS), in_=w1_rows)
                pitch = 768
            else:
                t = raw_pool.tile([P, 2048], BF16, name="raw", tag="raw")
                source = wv_rows[n // 2, n % 2] if kind == "wv" else rows[kind][n, :, :]
                pieces = 4 if unit == ("wv", 0) else 1
                width = 2048 // pieces
                for j in range(pieces):
                    nc.sync.dma_start(out=t[:, width * j:width * (j + 1)], in_=source[:, width * j:width * (j + 1)])
                pitch = 512
            words = t[:].bitcast(F32)
            raw[unit] = words
            columns[unit] = lambda s, g, u: words[:, pitch * s + 256 * g + u:pitch * s + 256 * (g + 1):2]

        stream = [("wv", 0), ("wv", 1), ("h", 0), ("h", 1), ("wv", 2), ("wv", 3), ("h", 2), ("h", 3)]
        for n in range(0, NSTEP, 2):
            stream.extend([("x", n), ("x", n + 1)])
            if n + 4 < NSTEP:
                stream.extend([("h", n + 4), ("h", n + 5)])

        def load_next(count):
            for unit in stream[:count]:
                load(unit)
            stream[:count] = []

        def sort(unit, copy=nc.vector.tensor_copy):
            if unit[0] == "w1":
                pitch = 768
                t = const.tile([P, 2 * pitch], F32, name="w1_srt")
            else:
                pitch = 512
                t = srt.tile([P, 2 * pitch], F32, name="srt", tag="srt")
            copy(
                out=t[:].rearrange("p (c u q) -> p c u q", u=2, q=P),
                in_=raw[unit].rearrange("p (c q u) -> p c u q", u=2, q=P),
            )
            columns[unit] = lambda s, g, u: t[:, pitch * s + 256 * g + P * u:pitch * s + 256 * g + P * (u + 1)]
            if unit[0] != "w1":
                load_next(1)

        def flip(units, pattern="SV"):
            n_bank = 0
            for unit in units:
                kind, n = unit
                groups = 3 if kind == "w1" else 2
                if kind in ("x", "h"):
                    pair = (kind, n // 2)
                    if pair not in grouped:
                        t = grp.tile([P, 4096], BF16, name=kind + "_grp", tag=kind + "_grp", align_bytes=64)
                        grouped[pair] = t
                    dest = grouped[pair][:, 2048 * (n % 2):2048 * (n % 2 + 1)]
                else:
                    t = const.tile([P, 1024 * groups], BF16, name="%s_grp%d" % unit, align_bytes=64)
                    grouped[unit] = t
                    dest = t[:]
                dest = dest.bitcast(F32).rearrange("p (g r u) -> p g r u", r=256, u=2)
                banks = []
                for g in range(groups):
                    bank = psum.tile([P, 2, 256], F32, name="bank", tag="bank")
                    banks.append(bank)
                if unit == ("wv", 0):
                    order = [(s, g, u) for s in range(2) for g in range(groups) for u in range(2)]
                    for s, g, u in order:
                        nc.tensor.transpose(banks[g][:, u, s * P:(s + 1) * P], columns[unit](s, g, u), ident[:])
                for g in range(groups):
                    if unit != ("wv", 0):
                        for u in range(2):
                            for s in range(2):
                                nc.tensor.transpose(banks[g][:, u, s * P:(s + 1) * P], columns[unit](s, g, u), ident[:])
                    copies[pattern[n_bank % len(pattern)]](out=dest[:, g], in_=banks[g][:].rearrange("p u r -> p r u"))
                    n_bank += 1

        def quantise_columns(src, codes, scales):
            nc.vector.quantize_mx(out=codes.bitcast(FP8X4), scales=scales, in_=src)

        def code_tiles(kind, unit):
            if kind in ("x", "h"):
                codes = cod.tile([P, 1024], U32, name=kind + "_c", tag=kind + "_c", align_bytes=64)
                scales = cod.tile([P, 1024], U8, name=kind + "_s", tag=kind + "_s", align_bytes=64)
            elif kind == "v":
                codes = cod.tile([P, 512], U32, name="v_c", tag="v_c", align_bytes=64)
                scales = cod.tile([P, 512], U8, name="v_s", tag="v_s", align_bytes=64)
            else:
                width = 768 if kind == "w1" else 512
                codes = const.tile([P, width], U32, name="%s_c%d" % unit, align_bytes=64)
                scales = const.tile([P, width], U8, name="%s_s%d" % unit, align_bytes=64)
            codes_of[unit] = (codes, scales)
            return codes, scales

        def quantise(unit):
            kind, n = unit
            codes, scales = code_tiles(kind, unit)
            if kind == "w1":
                for c in range(0, 768, 256):
                    quantise_columns(grouped[unit][:, 4 * c:4 * c + 1024], codes[:, c:c + 256], scales[:, c:c + 256])
            else:
                quantise_columns(grouped[unit][:], codes[:], scales[:])

        def quantise_half(pair, j):
            if pair not in codes_of:
                code_tiles(pair[0], pair)
            codes, scales = codes_of[pair]
            quantise_columns(grouped[pair][:, 2048 * j:2048 * (j + 1)], codes[:, 512 * j:512 * (j + 1)], scales[:, 512 * j:512 * (j + 1)])

        def quantise_views(i, k, s):
            unit = ("v", i)
            if unit not in codes_of:
                code_tiles("v", unit)
            codes, scales = codes_of[unit]
            c0 = P * (2 * k + s)
            quantise_columns(grouped[unit][:, 4 * c0:4 * (c0 + P)], codes[:, c0:c0 + P], scales[:, c0:c0 + P])

        def codes_at(kind, i, col, width):
            if kind in ("x", "h"):
                codes, scales = codes_of[(kind, i // 2)]
                col += 512 * (i % 2)
            else:
                codes, scales = codes_of[(kind, i)]
            return codes[:, col:col + width].bitcast(FP8X4), scales[:, col:col + width]

        def mx(acc, a, b, start, stop):
            nc.tensor.matmul_mx(out=acc, lhsT=a[0], lhsT_scale=a[1], rhs=b[0], rhs_scale=b[1], start=start, stop=stop)

        def views_tile(i):
            t = vgrp.tile([P, 2048], BF16, name="v_grp", tag="v_grp", align_bytes=64)
            grouped[("v", i)] = t

        def views(i, k, tiles=(0, 1)):
            if ("v", i) not in grouped:
                views_tile(i)
            dest = grouped[("v", i)][:].rearrange("p (k s r t) -> p k s r t", k=NS, s=2, t=4)
            for s in tiles:
                acc = psum.tile([P, 4, P], F32, name="v_acc", tag="bank")
                for t in range(4):
                    for g in range(2):
                        mx(acc[:, t, :], codes_at("wv", 2 * k + t // 2, 256 * g + P * (t % 2), P),
                           codes_at("h", i, 256 * g + P * s, P), g == 0, g == 1)
                nc.scalar.copy(out=dest[:, k, s], in_=acc[:].rearrange("p t r -> p r t"))

        def wide_views(i):
            flat = vgrp.tile([P, NS, 2, 256, 2], BF16, name="v_flat", tag="v_flat", bufs=2)
            flats[i] = flat
            for k in range(NS):
                for n in range(2):
                    acc = psum.tile([P, 2, 256], F32, name="v_acc", tag="bank")
                    for e in range(2):
                        for g in range(2):
                            mx(acc[:, e, :], codes_at("wv", 2 * k + n, 256 * g + P * e, P),
                               codes_at("h", i, 256 * g, 256), g == 0, g == 1)
                    nc.scalar.copy(out=flat[:, k, n], in_=acc[:].rearrange("p e r -> p r e"))

        def regroup(i):
            if i in flats:
                views_tile(i)
                nc.vector.tensor_copy(
                    out=grouped[("v", i)][:].bitcast(F32).rearrange("p (k r n) -> p k r n", k=NS, n=2),
                    in_=flats[i][:].rearrange("p k n r e -> p (k n r e)").bitcast(F32).rearrange("p (k n r) -> p k r n", k=NS, n=2),
                )

        def products(acc, i, s, subnets=(0, 1)):
            k0 = subnets[0]
            for g in range(2):
                mx(acc.rearrange("p k f -> p (k f)"), codes_at("x", i, 256 * g + P * s, P),
                   codes_at("w1", 0, 256 * g + P * k0, P * len(subnets)), g == 0, False)
            for k in subnets:
                mx(acc[:, k - k0, :], codes_at("v", i, P * (2 * k + s), P), codes_at("w1", 0, 512 + P * k, P),
                   False, k == subnets[-1])

        def finish_part(i, s, subnets=(0, 1)):
            k0, n = subnets[0], len(subnets)
            acc = psum.tile([P, n, SD], F32, name="o_part_acc", tag="bank")
            products(acc[:], i, s, subnets)
            o_part = res.tile([P, n, SD], F32, name="o_part", tag="o_part", bufs=6)
            nc.scalar.activation(out=o_part[:], in_=acc[:], func=SILU)
            nc.sync.dma_start(out=out_steps[i, :, k0:k0 + n, SD * s:SD * (s + 1)], in_=o_part[:])

        def finish(i):
            acc = psum.tile([P, 2, NS, SD], F32, name="o_acc", tag="bank")
            for s in range(2):
                products(acc[:, s], i, s)
            o_sb = res.tile([P, NS, 2, SD], F32, name="o_sb", tag="o_sb")
            nc.scalar.activation(out=o_sb[:], in_=acc[:].rearrange("p s k f -> p k s f"), func=SILU)
            nc.sync.dma_start(out=out_steps[i, :, :, :], in_=o_sb[:].rearrange("p k s f -> p k (s f)"))

        load_next(10)
        load(("w1", 0))
        load_next(2)

        flip([("wv", 0)])
        quantise(("wv", 0))
        flip([("wv", 1)])
        quantise(("wv", 1))
        flip([("h", 0)])
        quantise_half(("h", 0), 0)
        flip([("h", 1)])
        load_next(4)
        flip([("wv", 2)])
        load_next(1)
        sort(("wv", 3), nc.scalar.copy)
        views(0, 0)
        quantise_half(("h", 0), 1)
        quantise(("wv", 2))
        flip([("wv", 3)])

        sort(("h", 2))
        quantise(("wv", 3))
        sort(("h", 3), nc.scalar.copy)
        views(1, 0)
        flip([("h", 2), ("h", 3)])
        quantise_half(("h", 1), 0)
        views(0, 1)
        sort(("w1", 0), nc.scalar.copy)
        sort(("x", 0))
        sort(("x", 1))
        quantise(("v", 0))
        quantise_half(("h", 1), 1)
        sort(("h", 4))
        sort(("h", 5))
        views(1, 1)
        for a in range(2, NSTEP, 2):
            regroup(a - 1)
            units = [("x", a - 2), ("x", a - 1)]
            if a == 2:
                units.append(("w1", 0))
            if a + 2 < NSTEP:
                units.extend([("h", a + 2), ("h", a + 3)])
            else:
                units.extend([("x", a), ("x", a + 1)])
            flip(units, "SVSSVSSV")
            quantise(("x", a // 2 - 1))
            if a == 2:
                quantise(("w1", 0))
            quantise(("v", a - 1))
            later = []
            if a + 2 < NSTEP:
                later.extend([("x", a), ("x", a + 1)])
                later.extend([("h", a + 4), ("h", a + 5)] if a + 4 < NSTEP else [("x", a + 2), ("x", a + 3)])
            wide_views(a)
            for unit in later[:2]:
                sort(unit)
            regroup(a)
            finish(a - 2)
            for unit in later[2:]:
                sort(unit)
            if a + 2 < NSTEP:
                quantise(("h", a // 2 + 1))
                quantise(("v", a))
                wide_views(a + 1)
                finish(a - 1)
        quantise(("v", LAST - 1))
        quantise(("x", LAST // 2))
        for k in range(NS):
            views(LAST, k, (0,))
        finish(LAST - 2)
        for k in range(NS):
            quantise_views(LAST, k, 0)
        for k in range(NS):
            views(LAST, k, (1,))
        finish_part(LAST, 0)
        for k in range(NS):
            quantise_views(LAST, k, 1)
        finish_part(LAST - 1, 0)
        finish_part(LAST - 1, 1)
        finish_part(LAST, 1, (0,))
        finish_part(LAST, 1, (1,))
